import numpy as np
import ml_dtypes


def mxq(x, axis, fmt="e4m3"):
    dtype, down = {"e4m3": (ml_dtypes.float8_e4m3fn, 7), "e5m2": (ml_dtypes.float8_e5m2, 14)}[fmt]
    v = np.moveaxis(np.asarray(x, np.float32).astype(ml_dtypes.bfloat16).astype(np.float64), axis, -1)
    blocks = v.reshape(v.shape[:-1] + (-1, 32))
    amax = np.abs(blocks).max(-1, keepdims=True)
    byte = np.maximum(np.where(amax > 0, np.frexp(amax)[1] - 1 + 127, 0) - down, 1)
    scale = np.exp2(byte - 127.0)
    codes = (blocks / scale).astype(np.float32).astype(dtype).astype(np.float64)
    return np.moveaxis((codes * scale).reshape(v.shape), -1, axis)


WIDE = False


def mx_kscale(k):
    if not WIDE:
        return np.ones(k)
    levels = np.array([10, -10, 5, -5, 0])
    if k % 512:
        return np.exp2(np.random.permutation(np.resize(levels, k // 32))).repeat(32)
    a = np.empty((k // 512, 16))
    for p in range(k // 512):
        a[p, :8] = np.random.permutation(np.resize(levels, 8))
        for g in range(8):
            far = levels[np.abs(levels - a[p, g]) >= 10]
            a[p, g + 8] = far[np.random.randint(len(far))]
    return np.exp2(a.ravel()).repeat(32)


BF16 = ml_dtypes.bfloat16


def bf(x):
    return np.asarray(x, np.float32).astype(BF16)


def f64(x):
    return np.asarray(x).astype(np.float64)


B, L, H, U = 2, 4096, 512, 512
R_MIN, R_MAX = 0.9, 0.999


def setup_inputs():
    s, t = mx_kscale(H), mx_kscale(U)
    inputs = np.random.standard_normal((B, L, H)) * s
    Wi = np.random.standard_normal((U, H)) / np.sqrt(H) / s[None, :] * t[:, None]
    bi = np.random.standard_normal(U) * 0.03 * t
    Wo = np.random.standard_normal((H, U)) / np.sqrt(U) / t[None, :]
    bo = np.random.standard_normal(H) * 0.1
    r = np.random.uniform(size=U)
    nu_log = np.log(-0.5 * np.log(r * (R_MAX ** 2 - R_MIN ** 2) + R_MIN ** 2))
    gamma_log = np.log(np.sqrt(1.0 - np.exp(-np.exp(nu_log)) ** 2))
    params_log = np.stack([nu_log, gamma_log])
    return {"inputs": bf(inputs), "Wi": bf(Wi), "bi": bf(bi), "Wo": bf(Wo), "bo": bf(bo), "params_log": bf(params_log)}


def reference(inputs, Wi, bi, Wo, bo, params_log):
    u = (mxq(f64(inputs), 2, "e4m3") @ mxq(f64(Wi), 1, "e4m3").T) + f64(bi)
    params = np.exp(f64(params_log))
    nu, gamma = params[0], params[1]

    log2_L = int(np.ceil(np.log2(L)))
    pad_len = 2 ** log2_L - L
    x = np.pad(u, ((0, 0), (0, pad_len), (0, 0))) if pad_len else u
    Lp = 2 ** log2_L

    for i in range(1, log2_L + 1):
        l = 2 ** i
        x = x.reshape(B * Lp // l, l, U)
        x1, x2 = x[:, : l // 2], x[:, l // 2:]
        pos = np.arange(1, l // 2 + 1, dtype=np.float64)
        lambs = np.exp(-pos[:, None] * nu)
        x2 = x2 + lambs * x1[:, -1:]
        x = np.concatenate([x1, x2], axis=1).reshape(B, Lp, U)

    x = x[:, :L] * gamma
    return (mxq(x, 2, "e4m3") @ mxq(f64(Wo), 1, "e4m3").T) + f64(bo)

@@ -1,0 +1,360 @@
+from contextlib import ExitStack
+
+import concourse.mybir as mybir
+from concourse.masks import make_identity
+
+F32 = mybir.dt.float32
+BF16 = mybir.dt.bfloat16
+U32 = mybir.dt.uint32
+U8 = mybir.dt.uint8
+FP8X4 = mybir.dt.float8_e4m3fn_x4
+ACT = mybir.ActivationFunctionType
+ALU = mybir.AluOpType
+
+P = 128
+FEAT = 512
+CHAN = 512
+TOKENS = 8192
+SEQ = 4096
+HALF = 256
+SIZES = (256, 256) + (512,) * 15
+STARTS = tuple(sum(SIZES[:b]) for b in range(len(SIZES)))
+GROUPS = ((0,), (1,), (2,), (3, 4), (5, 6), (7, 8), (9, 10), (11, 12), (13, 14), (15,), (16,))
+G_TILES = (1, 1, 2) + (3, 3) * 4 + (2, 2) * 2 + (2, 0)
+S_SHARE = (0, 0, 128, 512, 512, 512, 512, 512, 768, 512, 384)
+ROW_BUFS = 12
+FLOPS = 2 * TOKENS * FEAT * CHAN * 2
+
+
+def tile_slru_t_kernel(tc, inputs, Wi, bi, Wo, bo, params_log, out):
+    nc = tc.nc
+    x_flat = inputs.flatten_outer_dims()
+    out_flat = out.flatten_outer_dims()
+    n_blocks = len(SIZES)
+    n_groups = len(GROUPS)
+    where = {}
+    group_len = []
+    for gi in range(n_groups):
+        off = 0
+        for b in GROUPS[gi]:
+            where[b] = (gi, off)
+            off += SIZES[b]
+        group_len.append(off)
+
+    def group(i):
+        return GROUPS[i] if 0 <= i < n_groups else ()
+
+    with ExitStack() as ctx:
+        const = ctx.enter_context(tc.tile_pool(name="const", bufs=1))
+        rows = ctx.enter_context(tc.tile_pool(name="rows", bufs=ROW_BUFS))
+        grp = ctx.enter_context(tc.tile_pool(name="grp", bufs=2))
+        xgp = ctx.enter_context(tc.tile_pool(name="xgp", bufs=3))
+        mxin = ctx.enter_context(tc.tile_pool(name="mxin", bufs=3))
+        upool = ctx.enter_context(tc.tile_pool(name="upool", bufs=2))
+        xpool = ctx.enter_context(tc.tile_pool(name="xpool", bufs=3))
+        opool = ctx.enter_context(tc.tile_pool(name="opool", bufs=4))
+        ps_l = ctx.enter_context(tc.psum_pool(name="ps_l", bufs=1))
+        ps = ctx.enter_context(tc.psum_pool(name="ps", bufs=7))
+        ctx.enter_context(tc.manual_schedule())
+
+        ident = const.tile([P, P], F32)
+        make_identity(nc, ident[:])
+        prow = const.tile([P, 4 * P], BF16)
+        nc.vector.memset(prow[:], 0.0)
+        lam_pad = const.tile([P, P], F32)
+        nc.vector.memset(lam_pad[:], 0.0)
+        bo_row = const.tile([P, FEAT], BF16)
+        nc.vector.memset(bo_row[:], 0.0)
+        ones = const.tile([P, P], BF16)
+        nc.vector.memset(ones[:], 1.0)
+        nc.scalar.dma_start(out=prow[0:2, :], in_=params_log)
+        nc.scalar.dma_start(out=prow[2:3, :], in_=bi.rearrange("(o f) -> o f", o=1))
+        nc.scalar.dma_start(out=bo_row[0:1, :], in_=bo.rearrange("(o f) -> o f", o=1))
+
+        x_sb = {}
+        loaded = [0]
+
+        def load_next():
+            b = loaded[0]
+            if b >= n_blocks:
+                return
+            loaded[0] = b + 1
+            pieces = SIZES[b] // P
+            x_tile = rows.tile([P, pieces * FEAT], BF16, tag="rows")
+            nc.sync.dma_start(
+                out=x_tile[:].rearrange("p (s h) -> p s h", s=pieces),
+                in_=x_flat[STARTS[b] : STARTS[b] + SIZES[b], :].rearrange("(s p) h -> p s h", p=P),
+            )
+            x_sb[b] = x_tile
+
+        wi_sb = rows.tile([P, 4 * FEAT], BF16, tag="rows")
+        for u in range(2):
+            nc.sync.dma_start(
+                out=wi_sb[:, u * 2 * FEAT : (u + 1) * 2 * FEAT].rearrange("p (e h) -> p e h", e=2),
+                in_=Wi.rearrange("(p e) h -> p e h", e=4)[:, 2 * u : 2 * u + 2, :],
+            )
+            load_next()
+        load_next()
+        wo_sb = rows.tile([P, 4 * CHAN], BF16, tag="rows")
+        nc.sync.dma_start(
+            out=wo_sb[:].rearrange("p (a c) -> p a c", a=4),
+            in_=Wo.rearrange("(a p) c -> p a c", p=P),
+        )
+        for k in range(ROW_BUFS - 5):
+            load_next()
+
+        warm = const.tile([P, 1], F32)
+        nc.scalar.activation(out=warm[:], in_=lam_pad[:, 0:1], func=ACT.Exp)
+
+        def transpose_half(src, half):
+            bank = ps.tile([P, 2, 2, P], F32, tag="bank")
+            src32 = src[:].bitcast(F32)
+            for s2 in range(2):
+                for u in range(2):
+                    first = (2 * half + s2) * 256
+                    nc.tensor.transpose(bank[:, s2, u, :], src32[:, first + u : first + 256 : 2], ident[:])
+            return bank
+
+        def copy_half(on_scalar, g_tile, half, bank):
+            g32 = g_tile[:].bitcast(F32).rearrange("p (c u) -> p c u", u=2)
+            dst = g32[:, half * HALF : (half + 1) * HALF, :].rearrange("p (s r) u -> p s r u", s=2)
+            view = bank[:].rearrange("p s u r -> p s r u")
+            if on_scalar:
+                nc.scalar.copy(out=dst, in_=view)
+            else:
+                nc.vector.tensor_copy(out=dst, in_=view)
+
+        def quantise(src, codes, scales):
+            nc.vector.quantize_mx(out=codes.bitcast(FP8X4), scales=scales, in_=src)
+
+        grouped = {}
+        in_mx = {}
+
+        def new_grouped(b):
+            g_tile = grp.tile([P, 4 * SIZES[b]], BF16, align_bytes=64, tag="grouped")
+            grouped[b] = g_tile
+
+        def q1(b):
+            in_codes = mxin.tile([P, SIZES[b]], U32, align_bytes=64, tag="in_codes")
+            in_scales = mxin.tile([P, SIZES[b]], U8, align_bytes=64, tag="in_scales")
+            quantise(grouped[b][:], in_codes[:], in_scales[:])
+            in_mx[b] = (in_codes, in_scales)
+
+        wi_codes = const.tile([P, CHAN], U32, align_bytes=64)
+        wi_scales = const.tile([P, CHAN], U8, align_bytes=64)
+        wo_codes = const.tile([P, FEAT], U32, align_bytes=64)
+        wo_scales = const.tile([P, FEAT], U8, align_bytes=64)
+
+        def quantise_weight_half(g_tile, codes, scales, h):
+            quantise(
+                g_tile[:, h * 4 * HALF : (h + 1) * 4 * HALF],
+                codes[:, h * HALF : (h + 1) * HALF],
+                scales[:, h * HALF : (h + 1) * HALF],
+            )
+
+        wi_g = grp.tile([P, 4 * CHAN], BF16, align_bytes=64, tag="grouped")
+        bank = transpose_half(wi_sb, 0)
+        copy_half(True, wi_g, 0, bank)
+        new_grouped(0)
+        bank = transpose_half(x_sb[0], 0)
+        copy_half(False, grouped[0], 0, bank)
+        load_next()
+        pbank = ps.tile([P, FEAT], F32, tag="bank")
+        for u in range(2):
+            nc.tensor.transpose(pbank[:, u * P : (u + 1) * P], prow[:].bitcast(F32)[:, u : 2 * P : 2], ident[:])
+        pwords = const.tile([P, 8], F32)
+        nc.vector.tensor_copy(
+            out=pwords[:].rearrange("p (r u) -> p r u", u=2),
+            in_=pbank[:, 0 : 2 * P].rearrange("p (u r) -> p r u", u=2)[:, 0:4, :],
+        )
+        pcol = pwords[:].bitcast(BF16)
+        nu = const.tile([P, 4], F32)
+        nc.scalar.activation(out=nu[:], in_=pcol[:, 0:4], func=ACT.Exp)
+        nc.scalar.activation(out=lam_pad[:, 0:4], in_=nu[:], func=ACT.Exp, scale=-1.0)
+        gam = const.tile([P, 4], F32)
+        nc.scalar.activation(out=gam[:], in_=pcol[:, 4:8], func=ACT.Exp)
+        bank = transpose_half(wi_sb, 1)
+        copy_half(True, wi_g, 1, bank)
+        load_next()
+        quantise_weight_half(wi_g, wi_codes, wi_scales, 0)
+        q1(0)
+        gbi = const.tile([P, 4], F32)
+        nc.vector.tensor_tensor(out=gbi[:], in0=gam[:], in1=pcol[:, 8:12], op=ALU.mult)
+        lbank = ps.tile([P, FEAT], F32, tag="bank")
+        nc.tensor.transpose(lbank[:, 0:P], lam_pad[:], ident[:])
+        lam_rows = const.tile([P, P], F32)
+        nc.vector.tensor_copy(out=lam_rows[:], in_=lbank[:, 0:P])
+        lam_ps = ps_l.tile([P, P], F32)
+        nc.tensor.transpose(lam_ps[:], lam_rows[:], ident[:])
+        quantise_weight_half(wi_g, wi_codes, wi_scales, 1)
+        new_grouped(1)
+        bank = transpose_half(x_sb[1], 0)
+        copy_half(False, grouped[1], 0, bank)
+        load_next()
+        q1(1)
+
+        bo32 = const.tile([P, FEAT], F32)
+        u_tiles = {}
+        xs_tiles = {}
+        xg = {}
+        x_mx = {}
+        o_tiles = {}
+
+        def phase1(c_blocks, a_blocks):
+            for b2 in a_blocks:
+                new_grouped(b2)
+                for h in range(SIZES[b2] // HALF):
+                    bank_a = transpose_half(x_sb[b2], h)
+                    copy_half(True, grouped[b2], h, bank_a)
+                load_next()
+            for b in c_blocks:
+                gi, off = where[b]
+                if gi not in u_tiles:
+                    u_sb = upool.tile([P, 4, group_len[gi]], F32, tag="u_sb")
+                    u_tiles[gi] = u_sb
+                for j in range(4):
+                    u_ps = ps.tile([P, SIZES[b]], F32, tag="bank")
+                    nc.tensor.matmul_mx(
+                        out=u_ps[:],
+                        lhsT=wi_codes[:, j * P : (j + 1) * P].bitcast(FP8X4),
+                        lhsT_scale=wi_scales[:, j * P : (j + 1) * P],
+                        rhs=in_mx[b][0][:].bitcast(FP8X4),
+                        rhs_scale=in_mx[b][1][:],
+                        start=True,
+                        stop=True,
+                    )
+                    nc.scalar.activation(
+                        out=u_tiles[gi][:, j, off : off + SIZES[b]],
+                        in_=u_ps[:],
+                        func=ACT.Identity,
+                        bias=gbi[:, j : j + 1],
+                        scale=gam[:, j : j + 1],
+                    )
+
+        def scan(gi):
+            n = group_len[gi]
+            xs = xpool.tile([P, 4, n], F32, tag="xs")
+            xs_tiles[gi] = xs
+            first = STARTS[GROUPS[gi][0]] % SEQ == 0
+            for j in range(4):
+                if first:
+                    start_value = 0.0
+                else:
+                    n_prev = group_len[gi - 1]
+                    start_value = xs_tiles[gi - 1][:, j, n_prev - 1 : n_prev]
+                nc.vector.tensor_tensor_scan(
+                    out=xs[:, j, :],
+                    data0=lam_ps[:, j : j + 1].to_broadcast([P, n]),
+                    data1=u_tiles[gi][:, j, :],
+                    initial=start_value,
+                    op0=ALU.mult,
+                    op1=ALU.add,
+                )
+
+        def regroup_scalar(gi):
+            n = group_len[gi]
+            lo = n - S_SHARE[gi]
+            if lo < n:
+                nc.scalar.copy(
+                    out=xg[gi][:, lo:n, :].rearrange("p (c i) j -> p c j i", i=4),
+                    in_=xs_tiles[gi][:, :, lo:n].rearrange("p j (c i) -> p c j i", i=4),
+                )
+
+        def regroup_gpsimd(gi):
+            n_g = group_len[gi] - S_SHARE[gi]
+            if n_g > 0:
+                nc.gpsimd.tensor_scalar(
+                    out=xg[gi][:, 0:n_g, :],
+                    in0=xs_tiles[gi][:, :, 0:n_g].rearrange("p j t -> p t j"),
+                    scalar1=1.0,
+                    scalar2=0.0,
+                    op0=ALU.mult,
+                    op1=ALU.add,
+                )
+
+        def q2(b):
+            x_codes = mxin.tile([P, SIZES[b]], U32, align_bytes=64, tag="x_codes")
+            x_scales = mxin.tile([P, SIZES[b]], U8, align_bytes=64, tag="x_scales")
+            gi, off = where[b]
+            quantise(xg[gi][:, off : off + SIZES[b], :].rearrange("p t j -> p (t j)"), x_codes[:], x_scales[:])
+            x_mx[b] = (x_codes, x_scales)
+
+        def store(b, t0, t1):
+            nc.sync.dma_start(
+                out=out_flat[STARTS[b] + t0 * P : STARTS[b] + t1 * P, :].rearrange("(s p) f -> p s f", p=P),
+                in_=o_tiles[b][:, t0:t1, :],
+            )
+
+        def v_tiles(b):
+            return SIZES[b] // P - G_TILES[b]
+
+        def stage2(blocks):
+            order = []
+            for b in blocks:
+                order.extend([(b, t) for t in range(v_tiles(b))])
+            for b in blocks:
+                order.extend([(b, t) for t in range(v_tiles(b), SIZES[b] // P)])
+            for b in blocks:
+                o_sb = opool.tile([P, SIZES[b] // P, FEAT], F32, tag="o_sb")
+                o_tiles[b] = o_sb
+            for b, t in order:
+                o_ps = ps.tile([P, FEAT], F32, tag="bank")
+                nc.tensor.matmul_mx(
+                    out=o_ps[:],
+                    lhsT=x_mx[b][0][:, t * P : (t + 1) * P].bitcast(FP8X4),
+                    lhsT_scale=x_mx[b][1][:, t * P : (t + 1) * P],
+                    rhs=wo_codes[:].bitcast(FP8X4),
+                    rhs_scale=wo_scales[:],
+                    start=True,
+                    stop=True,
+                )
+                if t < v_tiles(b):
+                    nc.vector.tensor_tensor(out=o_tiles[b][:, t, :], in0=o_ps[:], in1=bo32[:], op=ALU.add)
+                else:
+                    nc.scalar.copy(out=o_tiles[b][:, t, :], in_=o_ps[:])
+                if b == n_blocks - 1:
+                    store(b, t, t + 1)
+            for b in blocks:
+                if b < n_blocks - 1:
+                    store(b, 0, v_tiles(b))
+
+        def gp_add(b):
+            if G_TILES[b] > 0:
+                part = o_tiles[b][:, v_tiles(b) : SIZES[b] // P, :]
+                nc.gpsimd.tensor_tensor(
+                    out=part, in0=part, in1=bo32[:].unsqueeze(1).to_broadcast([P, G_TILES[b], FEAT]), op=ALU.add
+                )
+                store(b, v_tiles(b), SIZES[b] // P)
+
+        for s in range(-1, n_groups + 2):
+            a_blocks = group(s + 2) if s >= 0 else ()
+            phase1(group(s + 1), a_blocks)
+            if s == 0:
+                wo_g = xgp.tile([P, 4 * FEAT], BF16, align_bytes=64, tag="xg")
+                for h in range(2):
+                    bank = transpose_half(wo_sb, h)
+                    copy_half(True, wo_g, h, bank)
+                load_next()
+                bo_ps = ps.tile([P, FEAT], F32, tag="bank")
+                nc.tensor.matmul(out=bo_ps[:], lhsT=ones[:], rhs=bo_row[:], start=True, stop=True)
+                nc.scalar.copy(out=bo32[:], in_=bo_ps[:])
+            if 0 <= s < n_groups:
+                scan(s)
+                xg_tile = xgp.tile([P, group_len[s], 4], BF16, align_bytes=64, tag="xg")
+                xg[s] = xg_tile
+                regroup_scalar(s)
+            if 0 <= s - 1 < n_groups:
+                regroup_gpsimd(s - 1)
+            for b in group(s - 2):
+                gp_add(b)
+            done = group(s - 1)
+            if s == 1:
+                quantise(wo_g[:], wo_codes[:], wo_scales[:])
+            for b in done:
+                q2(b)
+            for b in a_blocks:
+                q1(b)
+            if 0 <= s < n_groups and S_SHARE[s] < group_len[s]:
+                nc.vector.memset(xg[s][:].rearrange("p t j -> p (t j)")[:, 0:2].bitcast(F32), 0.0)
+            if len(done) > 0:
+                stage2(done)

@@ -17,12 +17,25 @@ CHAN = 512
 TOKENS = 8192
 SEQ = 4096
 HALF = 256
-SIZES = (256, 256) + (512,) * 15
-STARTS = tuple(sum(SIZES[:b]) for b in range(len(SIZES)))
-GROUPS = ((0,), (1,), (2,), (3, 4), (5, 6), (7, 8), (9, 10), (11, 12), (13, 14), (15,), (16,))
-G_TILES = (1, 1, 2) + (3, 3) * 4 + (2, 2) * 2 + (2, 0)
-S_SHARE = (0, 0, 128, 512, 512, 512, 512, 512, 768, 512, 384)
-ROW_BUFS = 12
+BLOCK = 512
+GROUPS = (
+    (256, 0, 1),
+    (256, 0, 1),
+    (512, 128, 2),
+    (512, 256, 3),
+    (512, 256, 3),
+    (1024, 512, 3),
+    (1024, 512, 3),
+    (1024, 512, 3),
+    (1024, 512, 3),
+    (1024, 512, 3),
+    (512, 512, 2),
+    (256, 256, 0),
+    (128, 128, 0),
+    (128, 0, 0),
+)
+SHARED = (11, 12, 13)
+ROW_BUFS = 9
 FLOPS = 2 * TOKENS * FEAT * CHAN * 2
 
 
@@ -30,45 +43,77 @@ def tile_slru_t_kernel(tc, inputs, Wi, bi, Wo, bo, params_log, out):
     nc = tc.nc
     x_flat = inputs.flatten_outer_dims()
     out_flat = out.flatten_outer_dims()
-    n_blocks = len(SIZES)
     n_groups = len(GROUPS)
-    where = {}
+    sizes = []
+    starts = []
+    where = []
+    groups = []
     group_len = []
+    at = 0
+    in_blocks = []
+    in_sizes = []
+    in_starts = []
     for gi in range(n_groups):
+        n = GROUPS[gi][0]
+        members = []
         off = 0
-        for b in GROUPS[gi]:
-            where[b] = (gi, off)
-            off += SIZES[b]
-        group_len.append(off)
+        while off < n:
+            width = min(BLOCK, n - off)
+            members.append(len(sizes))
+            sizes.append(width)
+            starts.append(at + off)
+            where.append((gi, off))
+            if gi not in SHARED:
+                in_sizes.append(width)
+                in_starts.append(at + off)
+            elif gi == SHARED[0]:
+                in_sizes.append(sum(GROUPS[i][0] for i in SHARED))
+                in_starts.append(at + off)
+            off += width
+        in_blocks.append([len(in_sizes) - len(members) + i for i in range(len(members))] if gi not in SHARED[1:] else [])
+        groups.append(members)
+        group_len.append(n)
+        at += n
+    n_in = len(in_sizes)
 
     def group(i):
-        return GROUPS[i] if 0 <= i < n_groups else ()
+        return groups[i] if 0 <= i < n_groups else ()
+
+    def arrivals(i):
+        return in_blocks[i] if 0 <= i < n_groups else ()
+
+    def u_home(gi):
+        return SHARED[0] if gi in SHARED else gi
+
+    def u_columns(gi):
+        lo = sum(GROUPS[i][0] for i in SHARED if i < gi) if gi in SHARED else 0
+        return slice(lo, lo + group_len[gi])
 
     with ExitStack() as ctx:
         const = ctx.enter_context(tc.tile_pool(name="const", bufs=1))
         rows = ctx.enter_context(tc.tile_pool(name="rows", bufs=ROW_BUFS))
-        grp = ctx.enter_context(tc.tile_pool(name="grp", bufs=2))
+        grp = ctx.enter_context(tc.tile_pool(name="grp", bufs=3))
         xgp = ctx.enter_context(tc.tile_pool(name="xgp", bufs=3))
         mxin = ctx.enter_context(tc.tile_pool(name="mxin", bufs=3))
         upool = ctx.enter_context(tc.tile_pool(name="upool", bufs=2))
         xpool = ctx.enter_context(tc.tile_pool(name="xpool", bufs=3))
-        opool = ctx.enter_context(tc.tile_pool(name="opool", bufs=4))
+        opool = ctx.enter_context(tc.tile_pool(name="opool", bufs=6))
         ps_l = ctx.enter_context(tc.psum_pool(name="ps_l", bufs=1))
         ps = ctx.enter_context(tc.psum_pool(name="ps", bufs=7))
         ctx.enter_context(tc.manual_schedule())
 
+        par = const.tile([P, 8], BF16)
+        nc.scalar.dma_start(out=par[:].rearrange("p (v j) -> p v j", v=2), in_=params_log.rearrange("v (p j) -> p v j", j=4))
+        bi_sb = const.tile([P, 4], BF16)
+        nc.scalar.dma_start(out=bi_sb[:], in_=bi.rearrange("(p j) -> p j", j=4))
         ident = const.tile([P, P], F32)
         make_identity(nc, ident[:])
-        prow = const.tile([P, 4 * P], BF16)
-        nc.vector.memset(prow[:], 0.0)
         lam_pad = const.tile([P, P], F32)
         nc.vector.memset(lam_pad[:], 0.0)
         bo_row = const.tile([P, FEAT], BF16)
         nc.vector.memset(bo_row[:], 0.0)
         ones = const.tile([P, P], BF16)
         nc.vector.memset(ones[:], 1.0)
-        nc.scalar.dma_start(out=prow[0:2, :], in_=params_log)
-        nc.scalar.dma_start(out=prow[2:3, :], in_=bi.rearrange("(o f) -> o f", o=1))
         nc.scalar.dma_start(out=bo_row[0:1, :], in_=bo.rearrange("(o f) -> o f", o=1))
 
         x_sb = {}
@@ -76,14 +121,14 @@ def tile_slru_t_kernel(tc, inputs, Wi, bi, Wo, bo, params_log, out):
 
         def load_next():
             b = loaded[0]
-            if b >= n_blocks:
+            if b >= n_in:
                 return
             loaded[0] = b + 1
-            pieces = SIZES[b] // P
+            pieces = in_sizes[b] // P
             x_tile = rows.tile([P, pieces * FEAT], BF16, tag="rows")
             nc.sync.dma_start(
                 out=x_tile[:].rearrange("p (s h) -> p s h", s=pieces),
-                in_=x_flat[STARTS[b] : STARTS[b] + SIZES[b], :].rearrange("(s p) h -> p s h", p=P),
+                in_=x_flat[in_starts[b] : in_starts[b] + in_sizes[b], :].rearrange("(s p) h -> p s h", p=P),
             )
             x_sb[b] = x_tile
 
@@ -106,23 +151,30 @@ def tile_slru_t_kernel(tc, inputs, Wi, bi, Wo, bo, params_log, out):
         warm = const.tile([P, 1], F32)
         nc.scalar.activation(out=warm[:], in_=lam_pad[:, 0:1], func=ACT.Exp)
 
-        def transpose_half(src, half):
-            bank = ps.tile([P, 2, 2, P], F32, tag="bank")
+        def transpose_piece(src, first, count):
+            bank = ps.tile([P, count, 2, P], F32, tag="bank")
             src32 = src[:].bitcast(F32)
-            for s2 in range(2):
+            for s2 in range(count):
                 for u in range(2):
-                    first = (2 * half + s2) * 256
-                    nc.tensor.transpose(bank[:, s2, u, :], src32[:, first + u : first + 256 : 2], ident[:])
+                    w0 = (first + s2) * 256
+                    nc.tensor.transpose(bank[:, s2, u, :], src32[:, w0 + u : w0 + 256 : 2], ident[:])
             return bank
 
-        def copy_half(on_scalar, g_tile, half, bank):
+        def copy_piece(on_scalar, g_tile, first, count, bank):
             g32 = g_tile[:].bitcast(F32).rearrange("p (c u) -> p c u", u=2)
-            dst = g32[:, half * HALF : (half + 1) * HALF, :].rearrange("p (s r) u -> p s r u", s=2)
+            dst = g32[:, first * P : (first + count) * P, :].rearrange("p (s r) u -> p s r u", s=count)
             view = bank[:].rearrange("p s u r -> p s r u")
             if on_scalar:
                 nc.scalar.copy(out=dst, in_=view)
             else:
                 nc.vector.tensor_copy(out=dst, in_=view)
+
+        def transpose_and_copy(on_scalar, src, g_tile, n):
+            pieces = n // P
+            for first in range(0, pieces, 2):
+                count = min(2, pieces - first)
+                bank = transpose_piece(src, first, count)
+                copy_piece(on_scalar, g_tile, first, count, bank)
 
         def quantise(src, codes, scales):
             nc.vector.quantize_mx(out=codes.bitcast(FP8X4), scales=scales, in_=src)
@@ -130,13 +182,16 @@ def tile_slru_t_kernel(tc, inputs, Wi, bi, Wo, bo, params_log, out):
         grouped = {}
         in_mx = {}
 
-        def new_grouped(b):
-            g_tile = grp.tile([P, 4 * SIZES[b]], BF16, align_bytes=64, tag="grouped")
+        def bring(b, on_scalar, refill=1):
+            g_tile = grp.tile([P, 4 * in_sizes[b]], BF16, align_bytes=64, tag="grouped")
             grouped[b] = g_tile
+            transpose_and_copy(on_scalar, x_sb[b], g_tile, in_sizes[b])
+            for k in range(refill):
+                load_next()
 
         def q1(b):
-            in_codes = mxin.tile([P, SIZES[b]], U32, align_bytes=64, tag="in_codes")
-            in_scales = mxin.tile([P, SIZES[b]], U8, align_bytes=64, tag="in_scales")
+            in_codes = mxin.tile([P, in_sizes[b]], U32, align_bytes=64, tag="in_codes")
+            in_scales = mxin.tile([P, in_sizes[b]], U8, align_bytes=64, tag="in_scales")
             quantise(grouped[b][:], in_codes[:], in_scales[:])
             in_mx[b] = (in_codes, in_scales)
 
@@ -153,45 +208,33 @@ def tile_slru_t_kernel(tc, inputs, Wi, bi, Wo, bo, params_log, out):
             )
 
         wi_g = grp.tile([P, 4 * CHAN], BF16, align_bytes=64, tag="grouped")
-        bank = transpose_half(wi_sb, 0)
-        copy_half(True, wi_g, 0, bank)
-        new_grouped(0)
-        bank = transpose_half(x_sb[0], 0)
-        copy_half(False, grouped[0], 0, bank)
-        load_next()
-        pbank = ps.tile([P, FEAT], F32, tag="bank")
-        for u in range(2):
-            nc.tensor.transpose(pbank[:, u * P : (u + 1) * P], prow[:].bitcast(F32)[:, u : 2 * P : 2], ident[:])
-        pwords = const.tile([P, 8], F32)
-        nc.vector.tensor_copy(
-            out=pwords[:].rearrange("p (r u) -> p r u", u=2),
-            in_=pbank[:, 0 : 2 * P].rearrange("p (u r) -> p r u", u=2)[:, 0:4, :],
-        )
-        pcol = pwords[:].bitcast(BF16)
         nu = const.tile([P, 4], F32)
-        nc.scalar.activation(out=nu[:], in_=pcol[:, 0:4], func=ACT.Exp)
-        nc.scalar.activation(out=lam_pad[:, 0:4], in_=nu[:], func=ACT.Exp, scale=-1.0)
         gam = const.tile([P, 4], F32)
-        nc.scalar.activation(out=gam[:], in_=pcol[:, 4:8], func=ACT.Exp)
-        bank = transpose_half(wi_sb, 1)
-        copy_half(True, wi_g, 1, bank)
-        load_next()
+        gbi = const.tile([P, 4], F32)
+        bank = transpose_piece(wi_sb, 0, 2)
+        copy_piece(True, wi_g, 0, 2, bank)
+        nc.scalar.activation(out=nu[:], in_=par[:, 0:4], func=ACT.Exp)
+        nc.scalar.activation(out=gam[:], in_=par[:, 4:8], func=ACT.Exp)
+        bring(0, False, refill=0)
         quantise_weight_half(wi_g, wi_codes, wi_scales, 0)
         q1(0)
-        gbi = const.tile([P, 4], F32)
-        nc.vector.tensor_tensor(out=gbi[:], in0=gam[:], in1=pcol[:, 8:12], op=ALU.mult)
-        lbank = ps.tile([P, FEAT], F32, tag="bank")
-        nc.tensor.transpose(lbank[:, 0:P], lam_pad[:], ident[:])
-        lam_rows = const.tile([P, P], F32)
-        nc.vector.tensor_copy(out=lam_rows[:], in_=lbank[:, 0:P])
-        lam_ps = ps_l.tile([P, P], F32)
-        nc.tensor.transpose(lam_ps[:], lam_rows[:], ident[:])
-        quantise_weight_half(wi_g, wi_codes, wi_scales, 1)
-        new_grouped(1)
-        bank = transpose_half(x_sb[1], 0)
-        copy_half(False, grouped[1], 0, bank)
+        bank = transpose_piece(wi_sb, 2, 2)
+        copy_piece(True, wi_g, 2, 2, bank)
+        nc.scalar.activation(out=lam_pad[:, 0:4], in_=nu[:], func=ACT.Exp, scale=-1.0)
         load_next()
-        q1(1)
+        load_next()
+        nc.vector.tensor_tensor(out=gbi[:], in0=gam[:], in1=bi_sb[:], op=ALU.mult)
+        quantise_weight_half(wi_g, wi_codes, wi_scales, 1)
+        bring(1, False)
+
+        lam_ps = ps_l.tile([P, P], F32)
+
+        def lam_to_psum():
+            lbank = ps.tile([P, FEAT], F32, tag="bank")
+            nc.tensor.transpose(lbank[:, 0:P], lam_pad[:], ident[:])
+            lam_rows = const.tile([P, P], F32)
+            nc.scalar.copy(out=lam_rows[:], in_=lbank[:, 0:P])
+            nc.tensor.transpose(lam_ps[:], lam_rows[:], ident[:])
 
         bo32 = const.tile([P, FEAT], F32)
         u_tiles = {}
@@ -200,20 +243,17 @@ def tile_slru_t_kernel(tc, inputs, Wi, bi, Wo, bo, params_log, out):
         x_mx = {}
         o_tiles = {}
 
-        def phase1(c_blocks, a_blocks):
+        def phase1(gi, a_blocks):
+            c_blocks = arrivals(gi)
             for b2 in a_blocks:
-                new_grouped(b2)
-                for h in range(SIZES[b2] // HALF):
-                    bank_a = transpose_half(x_sb[b2], h)
-                    copy_half(True, grouped[b2], h, bank_a)
-                load_next()
+                bring(b2, True)
+            if len(c_blocks) > 0:
+                u_sb = upool.tile([P, 4, sum(in_sizes[b] for b in c_blocks)], F32, tag="u_sb")
+                u_tiles[gi] = u_sb
             for b in c_blocks:
-                gi, off = where[b]
-                if gi not in u_tiles:
-                    u_sb = upool.tile([P, 4, group_len[gi]], F32, tag="u_sb")
-                    u_tiles[gi] = u_sb
+                off = in_starts[b] - in_starts[c_blocks[0]]
                 for j in range(4):
-                    u_ps = ps.tile([P, SIZES[b]], F32, tag="bank")
+                    u_ps = ps.tile([P, in_sizes[b]], F32, tag="bank")
                     nc.tensor.matmul_mx(
                         out=u_ps[:],
                         lhsT=wi_codes[:, j * P : (j + 1) * P].bitcast(FP8X4),
@@ -224,28 +264,30 @@ def tile_slru_t_kernel(tc, inputs, Wi, bi, Wo, bo, params_log, out):
                         stop=True,
                     )
                     nc.scalar.activation(
-                        out=u_tiles[gi][:, j, off : off + SIZES[b]],
+                        out=u_sb[:, j, off : off + in_sizes[b]],
                         in_=u_ps[:],
                         func=ACT.Identity,
                         bias=gbi[:, j : j + 1],
                         scale=gam[:, j : j + 1],
                     )
 
-        def scan(gi):
+        def scan(gi, js):
             n = group_len[gi]
-            xs = xpool.tile([P, 4, n], F32, tag="xs")
-            xs_tiles[gi] = xs
-            first = STARTS[GROUPS[gi][0]] % SEQ == 0
-            for j in range(4):
+            if gi not in xs_tiles:
+                xs = xpool.tile([P, 4, n], F32, tag="xs")
+                xs_tiles[gi] = xs
+            first = starts[groups[gi][0]] % SEQ == 0
+            lam = lam_pad if gi < 2 else lam_ps
+            for j in js:
                 if first:
                     start_value = 0.0
                 else:
                     n_prev = group_len[gi - 1]
                     start_value = xs_tiles[gi - 1][:, j, n_prev - 1 : n_prev]
                 nc.vector.tensor_tensor_scan(
-                    out=xs[:, j, :],
-                    data0=lam_ps[:, j : j + 1].to_broadcast([P, n]),
-                    data1=u_tiles[gi][:, j, :],
+                    out=xs_tiles[gi][:, j, :],
+                    data0=lam[:, j : j + 1].to_broadcast([P, n]),
+                    data1=u_tiles[u_home(gi)][:, j, u_columns(gi)],
                     initial=start_value,
                     op0=ALU.mult,
                     op1=ALU.add,
@@ -253,7 +295,7 @@ def tile_slru_t_kernel(tc, inputs, Wi, bi, Wo, bo, params_log, out):
 
         def regroup_scalar(gi):
             n = group_len[gi]
-            lo = n - S_SHARE[gi]
+            lo = n - GROUPS[gi][1]
             if lo < n:
                 nc.scalar.copy(
                     out=xg[gi][:, lo:n, :].rearrange("p (c i) j -> p c j i", i=4),
@@ -261,8 +303,8 @@ def tile_slru_t_kernel(tc, inputs, Wi, bi, Wo, bo, params_log, out):
                 )
 
         def regroup_gpsimd(gi):
-            n_g = group_len[gi] - S_SHARE[gi]
-            if n_g > 0:
+            n_g = group_len[gi] - GROUPS[gi][1]
+            if n_g > 0 and gi < n_groups - 1:
                 nc.gpsimd.tensor_scalar(
                     out=xg[gi][:, 0:n_g, :],
                     in0=xs_tiles[gi][:, :, 0:n_g].rearrange("p j t -> p t j"),
@@ -273,29 +315,29 @@ def tile_slru_t_kernel(tc, inputs, Wi, bi, Wo, bo, params_log, out):
                 )
 
         def q2(b):
-            x_codes = mxin.tile([P, SIZES[b]], U32, align_bytes=64, tag="x_codes")
-            x_scales = mxin.tile([P, SIZES[b]], U8, align_bytes=64, tag="x_scales")
+            x_codes = mxin.tile([P, sizes[b]], U32, align_bytes=64, tag="x_codes")
+            x_scales = mxin.tile([P, sizes[b]], U8, align_bytes=64, tag="x_scales")
             gi, off = where[b]
-            quantise(xg[gi][:, off : off + SIZES[b], :].rearrange("p t j -> p (t j)"), x_codes[:], x_scales[:])
+            quantise(xg[gi][:, off : off + sizes[b], :].rearrange("p t j -> p (t j)"), x_codes[:], x_scales[:])
             x_mx[b] = (x_codes, x_scales)
 
         def store(b, t0, t1):
             nc.sync.dma_start(
-                out=out_flat[STARTS[b] + t0 * P : STARTS[b] + t1 * P, :].rearrange("(s p) f -> p s f", p=P),
+                out=out_flat[starts[b] + t0 * P : starts[b] + t1 * P, :].rearrange("(s p) f -> p s f", p=P),
                 in_=o_tiles[b][:, t0:t1, :],
             )
 
         def v_tiles(b):
-            return SIZES[b] // P - G_TILES[b]
+            return sizes[b] // P - GROUPS[where[b][0]][2]
 
         def stage2(blocks):
             order = []
             for b in blocks:
                 order.extend([(b, t) for t in range(v_tiles(b))])
             for b in blocks:
-                order.extend([(b, t) for t in range(v_tiles(b), SIZES[b] // P)])
+                order.extend([(b, t) for t in range(v_tiles(b), sizes[b] // P)])
             for b in blocks:
-                o_sb = opool.tile([P, SIZES[b] // P, FEAT], F32, tag="o_sb")
+                o_sb = opool.tile([P, sizes[b] // P, FEAT], F32, tag="o_sb")
                 o_tiles[b] = o_sb
             for b, t in order:
                 o_ps = ps.tile([P, FEAT], F32, tag="bank")
@@ -312,49 +354,60 @@ def tile_slru_t_kernel(tc, inputs, Wi, bi, Wo, bo, params_log, out):
                     nc.vector.tensor_tensor(out=o_tiles[b][:, t, :], in0=o_ps[:], in1=bo32[:], op=ALU.add)
                 else:
                     nc.scalar.copy(out=o_tiles[b][:, t, :], in_=o_ps[:])
-                if b == n_blocks - 1:
-                    store(b, t, t + 1)
             for b in blocks:
-                if b < n_blocks - 1:
+                if v_tiles(b) > 0:
                     store(b, 0, v_tiles(b))
 
         def gp_add(b):
-            if G_TILES[b] > 0:
-                part = o_tiles[b][:, v_tiles(b) : SIZES[b] // P, :]
+            g_tiles = GROUPS[where[b][0]][2]
+            if g_tiles > 0:
+                part = o_tiles[b][:, v_tiles(b) : sizes[b] // P, :]
                 nc.gpsimd.tensor_tensor(
-                    out=part, in0=part, in1=bo32[:].unsqueeze(1).to_broadcast([P, G_TILES[b], FEAT]), op=ALU.add
+                    out=part, in0=part, in1=bo32[:].unsqueeze(1).to_broadcast([P, g_tiles, FEAT]), op=ALU.add
                 )
-                store(b, v_tiles(b), SIZES[b] // P)
+                store(b, v_tiles(b), sizes[b] // P)
 
-        for s in range(-1, n_groups + 2):
-            a_blocks = group(s + 2) if s >= 0 else ()
-            phase1(group(s + 1), a_blocks)
+        last = n_groups - 1
+        phase1(0, ())
+        for s in range(n_groups):
+            a_blocks = arrivals(s + 2)
+            done = group(s - 1)
             if s == 0:
+                scan(0, (0,))
+                for b in arrivals(1):
+                    q1(b)
+                scan(0, (1, 2, 3))
+                phase1(1, a_blocks)
+                lam_to_psum()
                 wo_g = xgp.tile([P, 4 * FEAT], BF16, align_bytes=64, tag="xg")
-                for h in range(2):
-                    bank = transpose_half(wo_sb, h)
-                    copy_half(True, wo_g, h, bank)
+                transpose_and_copy(True, wo_sb, wo_g, FEAT)
                 load_next()
                 bo_ps = ps.tile([P, FEAT], F32, tag="bank")
                 nc.tensor.matmul(out=bo_ps[:], lhsT=ones[:], rhs=bo_row[:], start=True, stop=True)
                 nc.scalar.copy(out=bo32[:], in_=bo_ps[:])
-            if 0 <= s < n_groups:
-                scan(s)
-                xg_tile = xgp.tile([P, group_len[s], 4], BF16, align_bytes=64, tag="xg")
-                xg[s] = xg_tile
-                regroup_scalar(s)
-            if 0 <= s - 1 < n_groups:
+            else:
+                phase1(s + 1, a_blocks)
+                scan(s, range(4))
+            xg_tile = xgp.tile([P, group_len[s], 4], BF16, align_bytes=64, tag="xg")
+            xg[s] = xg_tile
+            regroup_scalar(s)
+            if s > 0:
                 regroup_gpsimd(s - 1)
             for b in group(s - 2):
                 gp_add(b)
-            done = group(s - 1)
             if s == 1:
                 quantise(wo_g[:], wo_codes[:], wo_scales[:])
             for b in done:
                 q2(b)
             for b in a_blocks:
                 q1(b)
-            if 0 <= s < n_groups and S_SHARE[s] < group_len[s]:
+            if GROUPS[s][1] < group_len[s] and s < last:
                 nc.vector.memset(xg[s][:].rearrange("p t j -> p (t j)")[:, 0:2].bitcast(F32), 0.0)
-            if len(done) > 0:
+            if s == last:
+                nc.vector.tensor_copy(out=xg[s][:], in_=xs_tiles[s][:].rearrange("p j t -> p t j"))
+                for b in group(s):
+                    q2(b)
+            if len(done) > 0 and s != last - 1:
                 stage2(done)
+        stage2(group(last - 2))
+        stage2(group(last))

@@ -19,20 +19,20 @@ SEQ = 4096
 HALF = 256
 BLOCK = 512
 GROUPS = (
-    (256, 0, 1),
-    (256, 0, 1),
-    (512, 128, 2),
-    (512, 256, 3),
-    (512, 256, 3),
-    (1024, 512, 3),
-    (1024, 512, 3),
-    (1024, 512, 3),
-    (1024, 512, 3),
-    (1024, 512, 3),
-    (512, 512, 2),
-    (256, 256, 0),
-    (128, 128, 0),
-    (128, 0, 0),
+    (256, 0, (1,)),
+    (256, 0, (1,)),
+    (512, 128, (2,)),
+    (512, 256, (3,)),
+    (512, 256, (3,)),
+    (1024, 512, (3, 4)),
+    (1024, 512, (3, 4)),
+    (1024, 512, (3, 4)),
+    (1024, 512, (3, 4)),
+    (1024, 512, (3, 4)),
+    (512, 512, (1,)),
+    (256, 256, (0,)),
+    (128, 128, (0,)),
+    (128, 0, (0,)),
 )
 SHARED = (11, 12, 13)
 ROW_BUFS = 9
@@ -322,13 +322,18 @@ def tile_slru_t_kernel(tc, inputs, Wi, bi, Wo, bo, params_log, out):
             x_mx[b] = (x_codes, x_scales)
 
         def store(b, t0, t1):
-            nc.sync.dma_start(
+            queue = nc.scalar if where[b][0] in SHARED else nc.sync
+            queue.dma_start(
                 out=out_flat[starts[b] + t0 * P : starts[b] + t1 * P, :].rearrange("(s p) f -> p s f", p=P),
                 in_=o_tiles[b][:, t0:t1, :],
             )
 
+        def g_tiles(b):
+            gi, off = where[b]
+            return GROUPS[gi][2][off // BLOCK]
+
         def v_tiles(b):
-            return sizes[b] // P - GROUPS[where[b][0]][2]
+            return sizes[b] // P - g_tiles(b)
 
         def stage2(blocks):
             order = []
@@ -359,13 +364,14 @@ def tile_slru_t_kernel(tc, inputs, Wi, bi, Wo, bo, params_log, out):
                     store(b, 0, v_tiles(b))
 
         def gp_add(b):
-            g_tiles = GROUPS[where[b][0]][2]
-            if g_tiles > 0:
-                part = o_tiles[b][:, v_tiles(b) : sizes[b] // P, :]
+            step = 4 if where[b][0] < SHARED[0] - 2 else 1
+            for t0 in range(v_tiles(b), sizes[b] // P, step):
+                t1 = min(t0 + step, sizes[b] // P)
+                part = o_tiles[b][:, t0:t1, :]
                 nc.gpsimd.tensor_tensor(
-                    out=part, in0=part, in1=bo32[:].unsqueeze(1).to_broadcast([P, g_tiles, FEAT]), op=ALU.add
+                    out=part, in0=part, in1=bo32[:].unsqueeze(1).to_broadcast([P, t1 - t0, FEAT]), op=ALU.add
                 )
-                store(b, v_tiles(b), sizes[b] // P)
+                store(b, t0, t1)
 
         last = n_groups - 1
         phase1(0, ())

@@ -24,12 +24,12 @@ GROUPS = (
     (512, 128, (2,)),
     (512, 256, (3,)),
     (512, 256, (3,)),
-    (1024, 512, (3, 4)),
-    (1024, 512, (3, 4)),
-    (1024, 512, (3, 4)),
-    (1024, 512, (3, 4)),
-    (1024, 512, (3, 4)),
-    (512, 512, (1,)),
+    (1024, 512, (3, 2)),
+    (1024, 512, (3, 2)),
+    (1024, 512, (3, 2)),
+    (1024, 512, (3, 2)),
+    (1024, 512, (3, 2)),
+    (512, 512, (2,)),
     (256, 256, (0,)),
     (128, 128, (0,)),
     (128, 0, (0,)),

@@ -364,14 +364,10 @@ def tile_slru_t_kernel(tc, inputs, Wi, bi, Wo, bo, params_log, out):
                     store(b, 0, v_tiles(b))
 
         def gp_add(b):
-            step = 4 if where[b][0] < SHARED[0] - 2 else 1
-            for t0 in range(v_tiles(b), sizes[b] // P, step):
-                t1 = min(t0 + step, sizes[b] // P)
-                part = o_tiles[b][:, t0:t1, :]
-                nc.gpsimd.tensor_tensor(
-                    out=part, in0=part, in1=bo32[:].unsqueeze(1).to_broadcast([P, t1 - t0, FEAT]), op=ALU.add
-                )
-                store(b, t0, t1)
+            for t in range(v_tiles(b), sizes[b] // P):
+                part = o_tiles[b][:, t, :]
+                nc.gpsimd.tensor_tensor(out=part, in0=part, in1=bo32[:], op=ALU.add)
+                store(b, t, t + 1)
 
         last = n_groups - 1
         phase1(0, ())

@@ -35,7 +35,7 @@ GROUPS = (
     (128, 0, (0,)),
 )
 SHARED = (11, 12, 13)
-ROW_BUFS = 9
+ROW_BUFS = 8
 FLOPS = 2 * TOKENS * FEAT * CHAN * 2
 
 
@@ -92,8 +92,9 @@ def tile_slru_t_kernel(tc, inputs, Wi, bi, Wo, bo, params_log, out):
     with ExitStack() as ctx:
         const = ctx.enter_context(tc.tile_pool(name="const", bufs=1))
         rows = ctx.enter_context(tc.tile_pool(name="rows", bufs=ROW_BUFS))
-        grp = ctx.enter_context(tc.tile_pool(name="grp", bufs=3))
+        grp = ctx.enter_context(tc.tile_pool(name="grp", bufs=2))
         xgp = ctx.enter_context(tc.tile_pool(name="xgp", bufs=3))
+        inmx = ctx.enter_context(tc.tile_pool(name="inmx", bufs=2))
         mxin = ctx.enter_context(tc.tile_pool(name="mxin", bufs=3))
         upool = ctx.enter_context(tc.tile_pool(name="upool", bufs=2))
         xpool = ctx.enter_context(tc.tile_pool(name="xpool", bufs=3))
@@ -161,7 +162,7 @@ def tile_slru_t_kernel(tc, inputs, Wi, bi, Wo, bo, params_log, out):
             return bank
 
         def copy_piece(on_scalar, g_tile, first, count, bank):
-            g32 = g_tile[:].bitcast(F32).rearrange("p (c u) -> p c u", u=2)
+            g32 = g_tile.bitcast(F32).rearrange("p (c u) -> p c u", u=2)
             dst = g32[:, first * P : (first + count) * P, :].rearrange("p (s r) u -> p s r u", s=count)
             view = bank[:].rearrange("p s u r -> p s r u")
             if on_scalar:
@@ -182,18 +183,25 @@ def tile_slru_t_kernel(tc, inputs, Wi, bi, Wo, bo, params_log, out):
         grouped = {}
         in_mx = {}
 
-        def bring(b, on_scalar, refill=1):
-            g_tile = grp.tile([P, 4 * in_sizes[b]], BF16, align_bytes=64, tag="grouped")
-            grouped[b] = g_tile
-            transpose_and_copy(on_scalar, x_sb[b], g_tile, in_sizes[b])
-            for k in range(refill):
-                load_next()
+        def bring(blocks, on_scalar, refill=1):
+            if len(blocks) > 0:
+                g_tile = grp.tile([P, 4 * sum(in_sizes[b] for b in blocks)], BF16, align_bytes=64, tag="grouped")
+                grouped[blocks[0]] = g_tile
+            for b in blocks:
+                lo = in_starts[b] - in_starts[blocks[0]]
+                transpose_and_copy(on_scalar, x_sb[b], g_tile[:, 4 * lo : 4 * (lo + in_sizes[b])], in_sizes[b])
+                for k in range(refill):
+                    load_next()
 
-        def q1(b):
-            in_codes = mxin.tile([P, in_sizes[b]], U32, align_bytes=64, tag="in_codes")
-            in_scales = mxin.tile([P, in_sizes[b]], U8, align_bytes=64, tag="in_scales")
-            quantise(grouped[b][:], in_codes[:], in_scales[:])
-            in_mx[b] = (in_codes, in_scales)
+        def q1(blocks):
+            if len(blocks) > 0:
+                n = sum(in_sizes[b] for b in blocks)
+                in_codes = inmx.tile([P, n], U32, align_bytes=64, tag="in_codes")
+                in_scales = inmx.tile([P, n], U8, align_bytes=64, tag="in_scales")
+                quantise(grouped[blocks[0]][:], in_codes[:], in_scales[:])
+            for b in blocks:
+                lo = in_starts[b] - in_starts[blocks[0]]
+                in_mx[b] = (in_codes[:, lo : lo + in_sizes[b]], in_scales[:, lo : lo + in_sizes[b]])
 
         wi_codes = const.tile([P, CHAN], U32, align_bytes=64)
         wi_scales = const.tile([P, CHAN], U8, align_bytes=64)
@@ -212,20 +220,20 @@ def tile_slru_t_kernel(tc, inputs, Wi, bi, Wo, bo, params_log, out):
         gam = const.tile([P, 4], F32)
         gbi = const.tile([P, 4], F32)
         bank = transpose_piece(wi_sb, 0, 2)
-        copy_piece(True, wi_g, 0, 2, bank)
+        copy_piece(True, wi_g[:], 0, 2, bank)
         nc.scalar.activation(out=nu[:], in_=par[:, 0:4], func=ACT.Exp)
         nc.scalar.activation(out=gam[:], in_=par[:, 4:8], func=ACT.Exp)
-        bring(0, False, refill=0)
+        bring(arrivals(0), False, refill=0)
         quantise_weight_half(wi_g, wi_codes, wi_scales, 0)
-        q1(0)
+        q1(arrivals(0))
         bank = transpose_piece(wi_sb, 2, 2)
-        copy_piece(True, wi_g, 2, 2, bank)
+        copy_piece(True, wi_g[:], 2, 2, bank)
         nc.scalar.activation(out=lam_pad[:, 0:4], in_=nu[:], func=ACT.Exp, scale=-1.0)
         load_next()
         load_next()
         nc.vector.tensor_tensor(out=gbi[:], in0=gam[:], in1=bi_sb[:], op=ALU.mult)
         quantise_weight_half(wi_g, wi_codes, wi_scales, 1)
-        bring(1, False)
+        bring(arrivals(1), False)
 
         lam_ps = ps_l.tile([P, P], F32)
 
@@ -245,8 +253,7 @@ def tile_slru_t_kernel(tc, inputs, Wi, bi, Wo, bo, params_log, out):
 
         def phase1(gi, a_blocks):
             c_blocks = arrivals(gi)
-            for b2 in a_blocks:
-                bring(b2, True)
+            bring(a_blocks, True)
             if len(c_blocks) > 0:
                 u_sb = upool.tile([P, 4, sum(in_sizes[b] for b in c_blocks)], F32, tag="u_sb")
                 u_tiles[gi] = u_sb
@@ -258,8 +265,8 @@ def tile_slru_t_kernel(tc, inputs, Wi, bi, Wo, bo, params_log, out):
                         out=u_ps[:],
                         lhsT=wi_codes[:, j * P : (j + 1) * P].bitcast(FP8X4),
                         lhsT_scale=wi_scales[:, j * P : (j + 1) * P],
-                        rhs=in_mx[b][0][:].bitcast(FP8X4),
-                        rhs_scale=in_mx[b][1][:],
+                        rhs=in_mx[b][0].bitcast(FP8X4),
+                        rhs_scale=in_mx[b][1],
                         start=True,
                         stop=True,
                     )
@@ -376,13 +383,12 @@ def tile_slru_t_kernel(tc, inputs, Wi, bi, Wo, bo, params_log, out):
             done = group(s - 1)
             if s == 0:
                 scan(0, (0,))
-                for b in arrivals(1):
-                    q1(b)
+                q1(arrivals(1))
                 scan(0, (1, 2, 3))
                 phase1(1, a_blocks)
                 lam_to_psum()
                 wo_g = xgp.tile([P, 4 * FEAT], BF16, align_bytes=64, tag="xg")
-                transpose_and_copy(True, wo_sb, wo_g, FEAT)
+                transpose_and_copy(True, wo_sb, wo_g[:], FEAT)
                 load_next()
                 bo_ps = ps.tile([P, FEAT], F32, tag="bank")
                 nc.tensor.matmul(out=bo_ps[:], lhsT=ones[:], rhs=bo_row[:], start=True, stop=True)
@@ -401,8 +407,7 @@ def tile_slru_t_kernel(tc, inputs, Wi, bi, Wo, bo, params_log, out):
                 quantise(wo_g[:], wo_codes[:], wo_scales[:])
             for b in done:
                 q2(b)
-            for b in a_blocks:
-                q1(b)
+            q1(a_blocks)
             if GROUPS[s][1] < group_len[s] and s < last:
                 nc.vector.memset(xg[s][:].rearrange("p t j -> p (t j)")[:, 0:2].bitcast(F32), 0.0)
             if s == last:

@@ -35,6 +35,7 @@ GROUPS = (
     (128, 0, (0,)),
 )
 SHARED = (11, 12, 13)
+FIRST_OUT = 2
 ROW_BUFS = 8
 FLOPS = 2 * TOKENS * FEAT * CHAN * 2
 
@@ -141,12 +142,13 @@ def tile_slru_t_kernel(tc, inputs, Wi, bi, Wo, bo, params_log, out):
             )
             load_next()
         load_next()
+        load_next()
         wo_sb = rows.tile([P, 4 * CHAN], BF16, tag="rows")
         nc.sync.dma_start(
             out=wo_sb[:].rearrange("p (a c) -> p a c", a=4),
             in_=Wo.rearrange("(a p) c -> p a c", p=P),
         )
-        for k in range(ROW_BUFS - 5):
+        for k in range(ROW_BUFS - 6):
             load_next()
 
         warm = const.tile([P, 1], F32)
@@ -362,12 +364,16 @@ def tile_slru_t_kernel(tc, inputs, Wi, bi, Wo, bo, params_log, out):
                     start=True,
                     stop=True,
                 )
-                if t < v_tiles(b):
+                if b == len(sizes) - 1:
+                    for f in (slice(0, FEAT // 2), slice(FEAT // 2, FEAT)):
+                        nc.vector.tensor_tensor(out=o_tiles[b][:, t, f], in0=o_ps[:, f], in1=bo32[:, f], op=ALU.add)
+                        nc.scalar.dma_start(out=out_flat[starts[b] : starts[b] + P, f], in_=o_tiles[b][:, t, f])
+                elif t < v_tiles(b):
                     nc.vector.tensor_tensor(out=o_tiles[b][:, t, :], in0=o_ps[:], in1=bo32[:], op=ALU.add)
                 else:
                     nc.scalar.copy(out=o_tiles[b][:, t, :], in_=o_ps[:])
             for b in blocks:
-                if v_tiles(b) > 0:
+                if v_tiles(b) > 0 and b < len(sizes) - 1:
                     store(b, 0, v_tiles(b))
 
         def gp_add(b):
@@ -378,32 +384,38 @@ def tile_slru_t_kernel(tc, inputs, Wi, bi, Wo, bo, params_log, out):
 
         last = n_groups - 1
         phase1(0, ())
+        done = []
         for s in range(n_groups):
             a_blocks = arrivals(s + 2)
-            done = group(s - 1)
+            added = done
+            if s == FIRST_OUT:
+                done = [b for gi in range(s) for b in group(gi)]
+            else:
+                done = group(s - 1) if s > FIRST_OUT else []
             if s == 0:
                 scan(0, (0,))
                 q1(arrivals(1))
                 scan(0, (1, 2, 3))
                 phase1(1, a_blocks)
                 lam_to_psum()
-                wo_g = xgp.tile([P, 4 * FEAT], BF16, align_bytes=64, tag="xg")
+            else:
+                phase1(s + 1, a_blocks)
+                scan(s, range(4))
+            if s == FIRST_OUT - 1:
+                wo_g = const.tile([P, 4 * FEAT], BF16, align_bytes=64)
                 transpose_and_copy(True, wo_sb, wo_g[:], FEAT)
                 load_next()
                 bo_ps = ps.tile([P, FEAT], F32, tag="bank")
                 nc.tensor.matmul(out=bo_ps[:], lhsT=ones[:], rhs=bo_row[:], start=True, stop=True)
                 nc.scalar.copy(out=bo32[:], in_=bo_ps[:])
-            else:
-                phase1(s + 1, a_blocks)
-                scan(s, range(4))
             xg_tile = xgp.tile([P, group_len[s], 4], BF16, align_bytes=64, tag="xg")
             xg[s] = xg_tile
             regroup_scalar(s)
             if s > 0:
                 regroup_gpsimd(s - 1)
-            for b in group(s - 2):
+            for b in added:
                 gp_add(b)
-            if s == 1:
+            if s == FIRST_OUT:
                 quantise(wo_g[:], wo_codes[:], wo_scales[:])
             for b in done:
                 q2(b)

from contextlib import ExitStack

import concourse.mybir as mybir
from concourse.masks import make_identity

F32 = mybir.dt.float32
BF16 = mybir.dt.bfloat16
U32 = mybir.dt.uint32
U8 = mybir.dt.uint8
FP8X4 = mybir.dt.float8_e4m3fn_x4
ACT = mybir.ActivationFunctionType
ALU = mybir.AluOpType

P = 128
FEAT = 512
CHAN = 512
TOKENS = 8192
SEQ = 4096
HALF = 256
BLOCK = 512
GROUPS = (
    (256, 0, (1,)),
    (256, 0, (1,)),
    (512, 128, (2,)),
    (512, 256, (3,)),
    (512, 256, (3,)),
    (1024, 512, (3, 2)),
    (1024, 512, (3, 2)),
    (1024, 512, (3, 2)),
    (1024, 512, (3, 2)),
    (1024, 512, (3, 2)),
    (512, 512, (2,)),
    (256, 256, (0,)),
    (128, 128, (0,)),
    (128, 0, (0,)),
)
SHARED = (11, 12, 13)
FIRST_OUT = 2
ROW_BUFS = 8
FLOPS = 2 * TOKENS * FEAT * CHAN * 2


def tile_slru_t_kernel(tc, inputs, Wi, bi, Wo, bo, params_log, out):
    nc = tc.nc
    x_flat = inputs.flatten_outer_dims()
    out_flat = out.flatten_outer_dims()
    n_groups = len(GROUPS)
    sizes = []
    starts = []
    where = []
    groups = []
    group_len = []
    at = 0
    in_blocks = []
    in_sizes = []
    in_starts = []
    for gi in range(n_groups):
        n = GROUPS[gi][0]
        members = []
        off = 0
        while off < n:
            width = min(BLOCK, n - off)
            members.append(len(sizes))
            sizes.append(width)
            starts.append(at + off)
            where.append((gi, off))
            if gi not in SHARED:
                in_sizes.append(width)
                in_starts.append(at + off)
            elif gi == SHARED[0]:
                in_sizes.append(sum(GROUPS[i][0] for i in SHARED))
                in_starts.append(at + off)
            off += width
        in_blocks.append([len(in_sizes) - len(members) + i for i in range(len(members))] if gi not in SHARED[1:] else [])
        groups.append(members)
        group_len.append(n)
        at += n
    n_in = len(in_sizes)

    def group(i):
        return groups[i] if 0 <= i < n_groups else ()

    def arrivals(i):
        return in_blocks[i] if 0 <= i < n_groups else ()

    def u_home(gi):
        return SHARED[0] if gi in SHARED else gi

    def u_columns(gi):
        lo = sum(GROUPS[i][0] for i in SHARED if i < gi) if gi in SHARED else 0
        return slice(lo, lo + group_len[gi])

    with ExitStack() as ctx:
        const = ctx.enter_context(tc.tile_pool(name="const", bufs=1))
        rows = ctx.enter_context(tc.tile_pool(name="rows", bufs=ROW_BUFS))
        grp = ctx.enter_context(tc.tile_pool(name="grp", bufs=2))
        xgp = ctx.enter_context(tc.tile_pool(name="xgp", bufs=3))
        inmx = ctx.enter_context(tc.tile_pool(name="inmx", bufs=2))
        mxin = ctx.enter_context(tc.tile_pool(name="mxin", bufs=3))
        upool = ctx.enter_context(tc.tile_pool(name="upool", bufs=2))
        xpool = ctx.enter_context(tc.tile_pool(name="xpool", bufs=3))
        opool = ctx.enter_context(tc.tile_pool(name="opool", bufs=6))
        ps_l = ctx.enter_context(tc.psum_pool(name="ps_l", bufs=1))
        ps = ctx.enter_context(tc.psum_pool(name="ps", bufs=7))
        ctx.enter_context(tc.manual_schedule())

        par = const.tile([P, 8], BF16)
        nc.scalar.dma_start(out=par[:].rearrange("p (v j) -> p v j", v=2), in_=params_log.rearrange("v (p j) -> p v j", j=4))
        bi_sb = const.tile([P, 4], BF16)
        nc.scalar.dma_start(out=bi_sb[:], in_=bi.rearrange("(p j) -> p j", j=4))
        ident = const.tile([P, P], F32)
        make_identity(nc, ident[:])
        lam_pad = const.tile([P, P], F32)
        nc.vector.memset(lam_pad[:], 0.0)
        bo_row = const.tile([P, FEAT], BF16)
        nc.vector.memset(bo_row[:], 0.0)
        ones = const.tile([P, P], BF16)
        nc.vector.memset(ones[:], 1.0)
        nc.scalar.dma_start(out=bo_row[0:1, :], in_=bo.rearrange("(o f) -> o f", o=1))

        x_sb = {}
        loaded = [0]

        def load_next():
            b = loaded[0]
            if b >= n_in:
                return
            loaded[0] = b + 1
            pieces = in_sizes[b] // P
            x_tile = rows.tile([P, pieces * FEAT], BF16, tag="rows")
            nc.sync.dma_start(
                out=x_tile[:].rearrange("p (s h) -> p s h", s=pieces),
                in_=x_flat[in_starts[b] : in_starts[b] + in_sizes[b], :].rearrange("(s p) h -> p s h", p=P),
            )
            x_sb[b] = x_tile

        wi_sb = rows.tile([P, 4 * FEAT], BF16, tag="rows")
        for u in range(2):
            nc.sync.dma_start(
                out=wi_sb[:, u * 2 * FEAT : (u + 1) * 2 * FEAT].rearrange("p (e h) -> p e h", e=2),
                in_=Wi.rearrange("(p e) h -> p e h", e=4)[:, 2 * u : 2 * u + 2, :],
            )
            load_next()
        load_next()
        load_next()
        wo_sb = rows.tile([P, 4 * CHAN], BF16, tag="rows")
        nc.sync.dma_start(
            out=wo_sb[:].rearrange("p (a c) -> p a c", a=4),
            in_=Wo.rearrange("(a p) c -> p a c", p=P),
        )
        for k in range(ROW_BUFS - 6):
            load_next()

        warm = const.tile([P, 1], F32)
        nc.scalar.activation(out=warm[:], in_=lam_pad[:, 0:1], func=ACT.Exp)

        def transpose_piece(src, first, count):
            bank = ps.tile([P, count, 2, P], F32, tag="bank")
            src32 = src[:].bitcast(F32)
            for s2 in range(count):
                for u in range(2):
                    w0 = (first + s2) * 256
                    nc.tensor.transpose(bank[:, s2, u, :], src32[:, w0 + u : w0 + 256 : 2], ident[:])
            return bank

        def copy_piece(on_scalar, g_tile, first, count, bank):
            g32 = g_tile.bitcast(F32).rearrange("p (c u) -> p c u", u=2)
            dst = g32[:, first * P : (first + count) * P, :].rearrange("p (s r) u -> p s r u", s=count)
            view = bank[:].rearrange("p s u r -> p s r u")
            if on_scalar:
                nc.scalar.copy(out=dst, in_=view)
            else:
                nc.vector.tensor_copy(out=dst, in_=view)

        def transpose_and_copy(on_scalar, src, g_tile, n):
            pieces = n // P
            for first in range(0, pieces, 2):
                count = min(2, pieces - first)
                bank = transpose_piece(src, first, count)
                copy_piece(on_scalar, g_tile, first, count, bank)

        def quantise(src, codes, scales):
            nc.vector.quantize_mx(out=codes.bitcast(FP8X4), scales=scales, in_=src)

        grouped = {}
        in_mx = {}

        def bring(blocks, on_scalar, refill=1):
            if len(blocks) > 0:
                g_tile = grp.tile([P, 4 * sum(in_sizes[b] for b in blocks)], BF16, align_bytes=64, tag="grouped")
                grouped[blocks[0]] = g_tile
            for b in blocks:
                lo = in_starts[b] - in_starts[blocks[0]]
                transpose_and_copy(on_scalar, x_sb[b], g_tile[:, 4 * lo : 4 * (lo + in_sizes[b])], in_sizes[b])
                for k in range(refill):
                    load_next()

        def q1(blocks):
            if len(blocks) > 0:
                n = sum(in_sizes[b] for b in blocks)
                in_codes = inmx.tile([P, n], U32, align_bytes=64, tag="in_codes")
                in_scales = inmx.tile([P, n], U8, align_bytes=64, tag="in_scales")
                quantise(grouped[blocks[0]][:], in_codes[:], in_scales[:])
            for b in blocks:
                lo = in_starts[b] - in_starts[blocks[0]]
                in_mx[b] = (in_codes[:, lo : lo + in_sizes[b]], in_scales[:, lo : lo + in_sizes[b]])

        wi_codes = const.tile([P, CHAN], U32, align_bytes=64)
        wi_scales = const.tile([P, CHAN], U8, align_bytes=64)
        wo_codes = const.tile([P, FEAT], U32, align_bytes=64)
        wo_scales = const.tile([P, FEAT], U8, align_bytes=64)

        def quantise_weight_half(g_tile, codes, scales, h):
            quantise(
                g_tile[:, h * 4 * HALF : (h + 1) * 4 * HALF],
                codes[:, h * HALF : (h + 1) * HALF],
                scales[:, h * HALF : (h + 1) * HALF],
            )

        wi_g = grp.tile([P, 4 * CHAN], BF16, align_bytes=64, tag="grouped")
        nu = const.tile([P, 4], F32)
        gam = const.tile([P, 4], F32)
        gbi = const.tile([P, 4], F32)
        bank = transpose_piece(wi_sb, 0, 2)
        copy_piece(True, wi_g[:], 0, 2, bank)
        nc.scalar.activation(out=nu[:], in_=par[:, 0:4], func=ACT.Exp)
        nc.scalar.activation(out=gam[:], in_=par[:, 4:8], func=ACT.Exp)
        bring(arrivals(0), False, refill=0)
        quantise_weight_half(wi_g, wi_codes, wi_scales, 0)
        q1(arrivals(0))
        bank = transpose_piece(wi_sb, 2, 2)
        copy_piece(True, wi_g[:], 2, 2, bank)
        nc.scalar.activation(out=lam_pad[:, 0:4], in_=nu[:], func=ACT.Exp, scale=-1.0)
        load_next()
        load_next()
        nc.vector.tensor_tensor(out=gbi[:], in0=gam[:], in1=bi_sb[:], op=ALU.mult)
        quantise_weight_half(wi_g, wi_codes, wi_scales, 1)
        bring(arrivals(1), False)

        lam_ps = ps_l.tile([P, P], F32)

        def lam_to_psum():
            lbank = ps.tile([P, FEAT], F32, tag="bank")
            nc.tensor.transpose(lbank[:, 0:P], lam_pad[:], ident[:])
            lam_rows = const.tile([P, P], F32)
            nc.scalar.copy(out=lam_rows[:], in_=lbank[:, 0:P])
            nc.tensor.transpose(lam_ps[:], lam_rows[:], ident[:])

        bo32 = const.tile([P, FEAT], F32)
        u_tiles = {}
        xs_tiles = {}
        xg = {}
        x_mx = {}
        o_tiles = {}

        def phase1(gi, a_blocks):
            c_blocks = arrivals(gi)
            bring(a_blocks, True)
            if len(c_blocks) > 0:
                u_sb = upool.tile([P, 4, sum(in_sizes[b] for b in c_blocks)], F32, tag="u_sb")
                u_tiles[gi] = u_sb
            for b in c_blocks:
                off = in_starts[b] - in_starts[c_blocks[0]]
                for j in range(4):
                    u_ps = ps.tile([P, in_sizes[b]], F32, tag="bank")
                    nc.tensor.matmul_mx(
                        out=u_ps[:],
                        lhsT=wi_codes[:, j * P : (j + 1) * P].bitcast(FP8X4),
                        lhsT_scale=wi_scales[:, j * P : (j + 1) * P],
                        rhs=in_mx[b][0].bitcast(FP8X4),
                        rhs_scale=in_mx[b][1],
                        start=True,
                        stop=True,
                    )
                    nc.scalar.activation(
                        out=u_sb[:, j, off : off + in_sizes[b]],
                        in_=u_ps[:],
                        func=ACT.Identity,
                        bias=gbi[:, j : j + 1],
                        scale=gam[:, j : j + 1],
                    )

        def scan(gi, js):
            n = group_len[gi]
            if gi not in xs_tiles:
                xs = xpool.tile([P, 4, n], F32, tag="xs")
                xs_tiles[gi] = xs
            first = starts[groups[gi][0]] % SEQ == 0
            lam = lam_pad if gi < 2 else lam_ps
            for j in js:
                if first:
                    start_value = 0.0
                else:
                    n_prev = group_len[gi - 1]
                    start_value = xs_tiles[gi - 1][:, j, n_prev - 1 : n_prev]
                nc.vector.tensor_tensor_scan(
                    out=xs_tiles[gi][:, j, :],
                    data0=lam[:, j : j + 1].to_broadcast([P, n]),
                    data1=u_tiles[u_home(gi)][:, j, u_columns(gi)],
                    initial=start_value,
                    op0=ALU.mult,
                    op1=ALU.add,
                )

        def regroup_scalar(gi):
            n = group_len[gi]
            lo = n - GROUPS[gi][1]
            if lo < n:
                nc.scalar.copy(
                    out=xg[gi][:, lo:n, :].rearrange("p (c i) j -> p c j i", i=4),
                    in_=xs_tiles[gi][:, :, lo:n].rearrange("p j (c i) -> p c j i", i=4),
                )

        def regroup_gpsimd(gi):
            n_g = group_len[gi] - GROUPS[gi][1]
            if n_g > 0 and gi < n_groups - 1:
                nc.gpsimd.tensor_scalar(
                    out=xg[gi][:, 0:n_g, :],
                    in0=xs_tiles[gi][:, :, 0:n_g].rearrange("p j t -> p t j"),
                    scalar1=1.0,
                    scalar2=0.0,
                    op0=ALU.mult,
                    op1=ALU.add,
                )

        def q2(b):
            x_codes = mxin.tile([P, sizes[b]], U32, align_bytes=64, tag="x_codes")
            x_scales = mxin.tile([P, sizes[b]], U8, align_bytes=64, tag="x_scales")
            gi, off = where[b]
            quantise(xg[gi][:, off : off + sizes[b], :].rearrange("p t j -> p (t j)"), x_codes[:], x_scales[:])
            x_mx[b] = (x_codes, x_scales)

        def store(b, t0, t1):
            queue = nc.scalar if where[b][0] in SHARED else nc.sync
            queue.dma_start(
                out=out_flat[starts[b] + t0 * P : starts[b] + t1 * P, :].rearrange("(s p) f -> p s f", p=P),
                in_=o_tiles[b][:, t0:t1, :],
            )

        def g_tiles(b):
            gi, off = where[b]
            return GROUPS[gi][2][off // BLOCK]

        def v_tiles(b):
            return sizes[b] // P - g_tiles(b)

        def stage2(blocks):
            order = []
            for b in blocks:
                order.extend([(b, t) for t in range(v_tiles(b))])
            for b in blocks:
                order.extend([(b, t) for t in range(v_tiles(b), sizes[b] // P)])
            for b in blocks:
                o_sb = opool.tile([P, sizes[b] // P, FEAT], F32, tag="o_sb")
                o_tiles[b] = o_sb
            for b, t in order:
                o_ps = ps.tile([P, FEAT], F32, tag="bank")
                nc.tensor.matmul_mx(
                    out=o_ps[:],
                    lhsT=x_mx[b][0][:, t * P : (t + 1) * P].bitcast(FP8X4),
                    lhsT_scale=x_mx[b][1][:, t * P : (t + 1) * P],
                    rhs=wo_codes[:].bitcast(FP8X4),
                    rhs_scale=wo_scales[:],
                    start=True,
                    stop=True,
                )
                if b == len(sizes) - 1:
                    for f in (slice(0, FEAT // 2), slice(FEAT // 2, FEAT)):
                        nc.vector.tensor_tensor(out=o_tiles[b][:, t, f], in0=o_ps[:, f], in1=bo32[:, f], op=ALU.add)
                        nc.scalar.dma_start(out=out_flat[starts[b] : starts[b] + P, f], in_=o_tiles[b][:, t, f])
                elif t < v_tiles(b):
                    nc.vector.tensor_tensor(out=o_tiles[b][:, t, :], in0=o_ps[:], in1=bo32[:], op=ALU.add)
                else:
                    nc.scalar.copy(out=o_tiles[b][:, t, :], in_=o_ps[:])
            for b in blocks:
                if v_tiles(b) > 0 and b < len(sizes) - 1:
                    store(b, 0, v_tiles(b))

        def gp_add(b):
            for t in range(v_tiles(b), sizes[b] // P):
                part = o_tiles[b][:, t, :]
                nc.gpsimd.tensor_tensor(out=part, in0=part, in1=bo32[:], op=ALU.add)
                store(b, t, t + 1)

        last = n_groups - 1
        phase1(0, ())
        done = []
        for s in range(n_groups):
            a_blocks = arrivals(s + 2)
            added = done
            if s == FIRST_OUT:
                done = [b for gi in range(s) for b in group(gi)]
            else:
                done = group(s - 1) if s > FIRST_OUT else []
            if s == 0:
                scan(0, (0,))
                q1(arrivals(1))
                scan(0, (1, 2, 3))
                phase1(1, a_blocks)
                lam_to_psum()
            else:
                phase1(s + 1, a_blocks)
                scan(s, range(4))
            if s == FIRST_OUT - 1:
                wo_g = const.tile([P, 4 * FEAT], BF16, align_bytes=64)
                transpose_and_copy(True, wo_sb, wo_g[:], FEAT)
                load_next()
                bo_ps = ps.tile([P, FEAT], F32, tag="bank")
                nc.tensor.matmul(out=bo_ps[:], lhsT=ones[:], rhs=bo_row[:], start=True, stop=True)
                nc.scalar.copy(out=bo32[:], in_=bo_ps[:])
            xg_tile = xgp.tile([P, group_len[s], 4], BF16, align_bytes=64, tag="xg")
            xg[s] = xg_tile
            regroup_scalar(s)
            if s > 0:
                regroup_gpsimd(s - 1)
            for b in added:
                gp_add(b)
            if s == FIRST_OUT:
                quantise(wo_g[:], wo_codes[:], wo_scales[:])
            for b in done:
                q2(b)
            q1(a_blocks)
            if GROUPS[s][1] < group_len[s] and s < last:
                nc.vector.memset(xg[s][:].rearrange("p t j -> p (t j)")[:, 0:2].bitcast(F32), 0.0)
            if s == last:
                nc.vector.tensor_copy(out=xg[s][:], in_=xs_tiles[s][:].rearrange("p j t -> p t j"))
                for b in group(s):
                    q2(b)
            if len(done) > 0 and s != last - 1:
                stage2(done)
        stage2(group(last - 2))
        stage2(group(last))
